import numpy as np
import ml_dtypes


def mxq(x, axis, fmt="e4m3"):
    dtype, down = {"e4m3": (ml_dtypes.float8_e4m3fn, 7), "e5m2": (ml_dtypes.float8_e5m2, 14)}[fmt]
    v = np.moveaxis(np.asarray(x, np.float32).astype(ml_dtypes.bfloat16).astype(np.float64), axis, -1)
    blocks = v.reshape(v.shape[:-1] + (-1, 32))
    amax = np.abs(blocks).max(-1, keepdims=True)
    byte = np.maximum(np.where(amax > 0, np.frexp(amax)[1] - 1 + 127, 0) - down, 1)
    scale = np.exp2(byte - 127.0)
    codes = (blocks / scale).astype(np.float32).astype(dtype).astype(np.float64)
    return np.moveaxis((codes * scale).reshape(v.shape), -1, axis)


WIDE = False


def mx_kscale(k):
    if not WIDE:
        return np.ones(k)
    levels = np.array([10, -10, 5, -5, 0])
    if k % 512:
        return np.exp2(np.random.permutation(np.resize(levels, k // 32))).repeat(32)
    a = np.empty((k // 512, 16))
    for p in range(k // 512):
        a[p, :8] = np.random.permutation(np.resize(levels, 8))
        for g in range(8):
            far = levels[np.abs(levels - a[p, g]) >= 10]
            a[p, g + 8] = far[np.random.randint(len(far))]
    return np.exp2(a.ravel()).repeat(32)


BF16 = ml_dtypes.bfloat16


def bf(x):
    return np.asarray(x, np.float32).astype(BF16)


def f64(x):
    return np.asarray(x).astype(np.float64)


B, D, S, N = 128, 1024, 4, 128
DS = D // S


def sigmoid(v):
    return 1.0 / (1.0 + np.exp(-v))


def setup_inputs():
    s = mx_kscale(D)
    t = np.maximum(1.0 + 2.0 * np.random.standard_normal((B, N, S)), 0.0) + np.maximum(1.0 + 2.0 * np.random.standard_normal((B, N, S)), 0.0)
    return {"a": bf(t * t / (t * t).sum(axis=1, keepdims=True)),
            "vr": bf(np.random.standard_normal((N, S, DS)) * 0.5 * np.sqrt(N) * s.reshape(S, DS)),
            "h": bf(np.random.standard_normal((B, D)) * s),
            "x2g": bf(np.random.standard_normal((B, D))),
            "w_g": bf(np.random.standard_normal((D, D)) / np.sqrt(D) / s),
            "b_g": bf(np.random.standard_normal(D) * 0.3),
            "bg": bf(1.0 + 0.1 * np.random.standard_normal(1))}


def reference(a, vr, h, x2g, w_g, b_g, bg):
    hf = f64(h)
    hh = (f64(a).transpose(2, 0, 1) @ f64(vr).transpose(1, 0, 2)).transpose(1, 0, 2).reshape(B, D)
    h2g = (mxq(hf, 1, "e4m3") @ mxq(f64(w_g), 1, "e4m3").T) + f64(b_g)
    g = sigmoid(f64(x2g) + h2g + f64(bg))
    return g * hh + (1.0 - g) * hf

@@ -1,0 +1,170 @@
+from contextlib import ExitStack
+
+import concourse.mybir as mybir
+from concourse.masks import make_identity
+
+F32 = mybir.dt.float32
+BF16 = mybir.dt.bfloat16
+U32 = mybir.dt.uint32
+U8 = mybir.dt.uint8
+FP8X4 = mybir.dt.float8_e4m3fn_x4
+ADD = mybir.AluOpType.add
+SUBTRACT = mybir.AluOpType.subtract
+MULT = mybir.AluOpType.mult
+SIGMOID = mybir.ActivationFunctionType.Sigmoid
+
+P = 128
+D = 1024
+SLICES = 4
+DS = D // SLICES
+PACK = 4
+K_PASS = P * PACK
+PASSES = D // K_PASS
+HALVES = 2
+GROUPS = D // P
+BIAS_RUN = D // P
+RUN = 2
+ROUNDS = GROUPS // RUN
+MULTIPLY_LAG = 1
+BLEND_LAG = 2
+
+FLOPS = 2 * P * D * D + 2 * P * P * D
+
+
+def tile_tpru_pb_s_kernel(tc, a, vr, h, x2g, w_g, b_g, bg, out):
+    nc = tc.nc
+    with ExitStack() as ctx:
+        keep = ctx.enter_context(tc.tile_pool(name="keep", bufs=1))
+        stage = ctx.enter_context(tc.tile_pool(name="stage", bufs=3))
+        flip = ctx.enter_context(tc.psum_pool(name="flip", bufs=4))
+        roles = ctx.enter_context(tc.psum_pool(name="roles", bufs=1))
+        gate = ctx.enter_context(tc.psum_pool(name="gate", bufs=2))
+
+        b_runs = keep.tile([P, BIAS_RUN], BF16)
+        nc.sync.dma_start(out=b_runs[:], in_=b_g.rearrange("(p m) -> p m", m=BIAS_RUN))
+        bg_bf = keep.tile([P, 1], BF16)
+        nc.sync.dma_start(out=bg_bf[:], in_=bg.partition_broadcast(P))
+        x_sb = keep.tile([P, D], BF16)
+        nc.sync.dma_start(out=x_sb[:], in_=x2g)
+        h_sb = keep.tile([P, D], BF16)
+        nc.sync.dma_start(out=h_sb[:], in_=h)
+        a_sb = keep.tile([P, P, SLICES], BF16)
+        nc.sync.dma_start(out=a_sb[:], in_=a)
+        vr_sb = keep.tile([P, SLICES, DS], BF16)
+        nc.sync.dma_start(out=vr_sb[:], in_=vr)
+        w_sb = []
+        for grp in range(GROUPS):
+            w_rows = keep.tile([P, D], BF16, name="w_rows%d" % grp)
+            nc.sync.dma_start(out=w_rows[:], in_=w_g[grp * P : (grp + 1) * P, :])
+            w_sb.append(w_rows)
+
+        ident_bf = keep.tile([P, P], BF16)
+        make_identity(nc, ident_bf[:])
+        ident_f32 = keep.tile([P, P], F32)
+        make_identity(nc, ident_f32[:])
+        zero_col = keep.tile([P, 1], F32)
+        nc.vector.memset(zero_col[:], 0.0)
+        half_col = keep.tile([P, 1], F32)
+        nc.scalar.activation(out=half_col[:], in_=zero_col[:], func=SIGMOID)
+
+        bias_flip = flip.tile([P, BIAS_RUN, P], BF16, tag="flip")
+        for m in range(BIAS_RUN):
+            nc.tensor.transpose(bias_flip[:, m, :], b_runs[:, m : m + 1].to_broadcast([P, P]), ident_bf[:])
+        bg_f32 = keep.tile([P, 1], F32)
+        nc.vector.tensor_copy(out=bg_f32[:], in_=bg_bf[:])
+        pre = keep.tile([P, D], F32)
+        nc.vector.scalar_tensor_tensor(
+            out=pre[:].rearrange("b (p m) -> b p m", m=BIAS_RUN),
+            in0=bias_flip[:].rearrange("b m p -> b p m"),
+            scalar=bg_f32[:, 0:1],
+            in1=x_sb[:].rearrange("b (p m) -> b p m", m=BIAS_RUN),
+            op0=ADD,
+            op1=ADD,
+        )
+
+        h_words = h_sb[:].bitcast(F32)
+        h_flip = flip.tile([P, PASSES, HALVES, P], F32, tag="flip")
+        for c in range(PASSES):
+            for u in range(HALVES):
+                words = slice(c * HALVES * P + u, (c + 1) * HALVES * P, HALVES)
+                nc.tensor.transpose(h_flip[:, c, u, :], h_words[:, words], ident_f32[:])
+        h_grouped = keep.tile([P, PASSES, P, PACK], BF16, align_bytes=64)
+        nc.scalar.copy(out=h_grouped[:].bitcast(F32), in_=h_flip[:].rearrange("p c u b -> p c b u"))
+        h_codes = keep.tile([P, PASSES * P], U32, align_bytes=64)
+        h_scales = keep.tile([P, PASSES * P], U8, align_bytes=64)
+        nc.vector.quantize_mx(
+            out=h_codes[:].bitcast(FP8X4),
+            scales=h_scales[:],
+            in_=h_grouped[:].rearrange("p c b t -> p (c b t)"),
+        )
+
+        a_flip = flip.tile([P, SLICES, P], BF16, tag="flip")
+        for s in range(SLICES):
+            nc.tensor.transpose(a_flip[:, s, :], a_sb[:, :, s], ident_bf[:])
+        a_t = keep.tile([P, SLICES, P], BF16)
+        nc.scalar.copy(out=a_t[:], in_=a_flip[:])
+        diff = keep.tile([P, D], F32)
+        for bank in range(SLICES // 2):
+            hh = roles.tile([P, 2, DS], F32, name="hh%d" % bank)
+            for i in range(2):
+                s = 2 * bank + i
+                nc.tensor.matmul(out=hh[:, i, :], lhsT=a_t[:, s, :], rhs=vr_sb[:, s, :], start=True, stop=True)
+            cols = slice(2 * bank * DS, 2 * (bank + 1) * DS)
+            nc.vector.tensor_tensor(
+                out=diff[:, cols], in0=hh[:].rearrange("b i d -> b (i d)"), in1=h_sb[:, cols], op=SUBTRACT
+            )
+
+        w_codes = keep.tile([P, GROUPS, PASSES * P], U32, align_bytes=64)
+        w_scales = keep.tile([P, GROUPS, PASSES * P], U8, align_bytes=64)
+        z = keep.tile([P, D], F32)
+        g = keep.tile([P, D], F32)
+        blend = keep.tile([P, D], F32)
+        result = keep.tile([P, D], F32)
+
+        def quantise_group(grp):
+            w_words = w_sb[grp][:].bitcast(F32)
+            w_flip = flip.tile([P, PASSES, HALVES, P], F32, tag="flip", name="w_flip")
+            for c in range(PASSES):
+                for u in range(HALVES):
+                    words = slice(c * HALVES * P + u, (c + 1) * HALVES * P, HALVES)
+                    nc.tensor.transpose(w_flip[:, c, u, :], w_words[:, words], ident_f32[:])
+            w_grouped = stage.tile([P, PASSES, P, PACK], BF16, align_bytes=64, name="w_grouped")
+            nc.scalar.copy(out=w_grouped[:].bitcast(F32), in_=w_flip[:].rearrange("p c u o -> p c o u"))
+            nc.vector.quantize_mx(
+                out=w_codes[:, grp, :].bitcast(FP8X4),
+                scales=w_scales[:, grp, :],
+                in_=w_grouped[:].rearrange("p c o t -> p (c o t)"),
+            )
+
+        def multiply_group(grp):
+            cols = slice(grp * P, (grp + 1) * P)
+            h2g = gate.tile([P, P], F32, name="h2g")
+            for c in range(PASSES):
+                nc.tensor.matmul_mx(
+                    out=h2g[:],
+                    lhsT=h_codes[:, c * P : (c + 1) * P].bitcast(FP8X4),
+                    lhsT_scale=h_scales[:, c * P : (c + 1) * P],
+                    rhs=w_codes[:, grp, c * P : (c + 1) * P].bitcast(FP8X4),
+                    rhs_scale=w_scales[:, grp, c * P : (c + 1) * P],
+                    start=(c == 0),
+                    stop=(c == PASSES - 1),
+                )
+            nc.vector.tensor_tensor(out=z[:, cols], in0=h2g[:], in1=pre[:, cols], op=ADD)
+
+        def blend_group(grp):
+            cols = slice(grp * P, (grp + 1) * P)
+            nc.scalar.activation(out=g[:, cols], in_=z[:, cols], func=SIGMOID)
+            nc.vector.tensor_tensor(out=blend[:, cols], in0=g[:, cols], in1=diff[:, cols], op=MULT)
+            nc.vector.tensor_tensor(out=result[:, cols], in0=blend[:, cols], in1=h_sb[:, cols], op=ADD)
+            nc.sync.dma_start(out=out[:, cols], in_=result[:, cols])
+
+        for rnd in range(ROUNDS + BLEND_LAG):
+            for i in range(RUN):
+                if rnd < ROUNDS:
+                    quantise_group(rnd * RUN + i)
+            for i in range(RUN):
+                if 0 <= rnd - MULTIPLY_LAG < ROUNDS:
+                    multiply_group((rnd - MULTIPLY_LAG) * RUN + i)
+            for i in range(RUN):
+                if 0 <= rnd - BLEND_LAG:
+                    blend_group((rnd - BLEND_LAG) * RUN + i)

@@ -22,11 +22,7 @@ K_PASS = P * PACK
 PASSES = D // K_PASS
 HALVES = 2
 GROUPS = D // P
-BIAS_RUN = D // P
-RUN = 2
-ROUNDS = GROUPS // RUN
-MULTIPLY_LAG = 1
-BLEND_LAG = 2
+BIAS_WORDS = D // P // 2
 
 FLOPS = 2 * P * D * D + 2 * P * P * D
 
@@ -35,59 +31,67 @@ def tile_tpru_pb_s_kernel(tc, a, vr, h, x2g, w_g, b_g, bg, out):
     nc = tc.nc
     with ExitStack() as ctx:
         keep = ctx.enter_context(tc.tile_pool(name="keep", bufs=1))
-        stage = ctx.enter_context(tc.tile_pool(name="stage", bufs=3))
+        stage = ctx.enter_context(tc.tile_pool(name="stage", bufs=4))
         flip = ctx.enter_context(tc.psum_pool(name="flip", bufs=4))
         roles = ctx.enter_context(tc.psum_pool(name="roles", bufs=1))
-        gate = ctx.enter_context(tc.psum_pool(name="gate", bufs=2))
+        gate = ctx.enter_context(tc.psum_pool(name="gate", bufs=3))
 
-        b_runs = keep.tile([P, BIAS_RUN], BF16)
-        nc.sync.dma_start(out=b_runs[:], in_=b_g.rearrange("(p m) -> p m", m=BIAS_RUN))
+        ident_f32 = keep.tile([P, P], F32)
+        make_identity(nc, ident_f32[:])
+        ident_bf = keep.tile([P, P], BF16)
+        make_identity(nc, ident_bf[:])
+
+        ctx.enter_context(tc.manual_schedule())
+
+        b_runs = keep.tile([P, 2 * BIAS_WORDS], BF16)
+        nc.sync.dma_start(out=b_runs[:], in_=b_g.rearrange("(p m) -> p m", m=2 * BIAS_WORDS))
         bg_bf = keep.tile([P, 1], BF16)
         nc.sync.dma_start(out=bg_bf[:], in_=bg.partition_broadcast(P))
-        x_sb = keep.tile([P, D], BF16)
-        nc.sync.dma_start(out=x_sb[:], in_=x2g)
         h_sb = keep.tile([P, D], BF16)
         nc.sync.dma_start(out=h_sb[:], in_=h)
+        x_sb = keep.tile([P, D], BF16)
+        nc.sync.dma_start(out=x_sb[:], in_=x2g)
         a_sb = keep.tile([P, P, SLICES], BF16)
         nc.sync.dma_start(out=a_sb[:], in_=a)
         vr_sb = keep.tile([P, SLICES, DS], BF16)
-        nc.sync.dma_start(out=vr_sb[:], in_=vr)
         w_sb = []
         for grp in range(GROUPS):
             w_rows = keep.tile([P, D], BF16, name="w_rows%d" % grp)
             nc.sync.dma_start(out=w_rows[:], in_=w_g[grp * P : (grp + 1) * P, :])
             w_sb.append(w_rows)
+            if grp == 0:
+                nc.sync.dma_start(out=vr_sb[:], in_=vr)
 
-        ident_bf = keep.tile([P, P], BF16)
-        make_identity(nc, ident_bf[:])
-        ident_f32 = keep.tile([P, P], F32)
-        make_identity(nc, ident_f32[:])
         zero_col = keep.tile([P, 1], F32)
         nc.vector.memset(zero_col[:], 0.0)
         half_col = keep.tile([P, 1], F32)
         nc.scalar.activation(out=half_col[:], in_=zero_col[:], func=SIGMOID)
+        minus_ident = keep.tile([P, P], BF16)
+        nc.vector.tensor_scalar(out=minus_ident[:], in0=ident_bf[:], scalar1=-1.0, scalar2=None, op0=MULT)
 
-        bias_flip = flip.tile([P, BIAS_RUN, P], BF16, tag="flip")
-        for m in range(BIAS_RUN):
-            nc.tensor.transpose(bias_flip[:, m, :], b_runs[:, m : m + 1].to_broadcast([P, P]), ident_bf[:])
+        b_words = b_runs[:].bitcast(F32)
+        bias_flip = flip.tile([P, BIAS_WORDS, P], F32, tag="flip")
+        for m in range(BIAS_WORDS):
+            nc.tensor.transpose(bias_flip[:, m, :], b_words[:, m : m + 1].to_broadcast([P, P]), ident_f32[:])
         bg_f32 = keep.tile([P, 1], F32)
         nc.vector.tensor_copy(out=bg_f32[:], in_=bg_bf[:])
         pre = keep.tile([P, D], F32)
-        nc.vector.scalar_tensor_tensor(
-            out=pre[:].rearrange("b (p m) -> b p m", m=BIAS_RUN),
-            in0=bias_flip[:].rearrange("b m p -> b p m"),
-            scalar=bg_f32[:, 0:1],
-            in1=x_sb[:].rearrange("b (p m) -> b p m", m=BIAS_RUN),
-            op0=ADD,
-            op1=ADD,
+        nc.vector.tensor_tensor(
+            out=pre[:].rearrange("b (p m e) -> b p m e", m=BIAS_WORDS, e=2),
+            in0=bias_flip[:].rearrange("b m p -> b (m p)").bitcast(BF16).rearrange("b (m p e) -> b p m e", m=BIAS_WORDS, e=2),
+            in1=x_sb[:].rearrange("b (p m e) -> b p m e", m=BIAS_WORDS, e=2),
+            op=ADD,
         )
 
-        h_words = h_sb[:].bitcast(F32)
+        def transpose_words(rows, banked):
+            words = rows[:].bitcast(F32)
+            for c in range(PASSES):
+                for u in range(HALVES):
+                    picked = slice(c * HALVES * P + u, (c + 1) * HALVES * P, HALVES)
+                    nc.tensor.transpose(banked[:, c, u, :], words[:, picked], ident_f32[:])
+
         h_flip = flip.tile([P, PASSES, HALVES, P], F32, tag="flip")
-        for c in range(PASSES):
-            for u in range(HALVES):
-                words = slice(c * HALVES * P + u, (c + 1) * HALVES * P, HALVES)
-                nc.tensor.transpose(h_flip[:, c, u, :], h_words[:, words], ident_f32[:])
+        transpose_words(h_sb, h_flip)
         h_grouped = keep.tile([P, PASSES, P, PACK], BF16, align_bytes=64)
         nc.scalar.copy(out=h_grouped[:].bitcast(F32), in_=h_flip[:].rearrange("p c u b -> p c b u"))
         h_codes = keep.tile([P, PASSES * P], U32, align_bytes=64)
@@ -98,20 +102,32 @@ def tile_tpru_pb_s_kernel(tc, a, vr, h, x2g, w_g, b_g, bg, out):
             in_=h_grouped[:].rearrange("p c b t -> p (c b t)"),
         )
 
-        a_flip = flip.tile([P, SLICES, P], BF16, tag="flip")
-        for s in range(SLICES):
-            nc.tensor.transpose(a_flip[:, s, :], a_sb[:, :, s], ident_bf[:])
         a_t = keep.tile([P, SLICES, P], BF16)
-        nc.scalar.copy(out=a_t[:], in_=a_flip[:])
-        diff = keep.tile([P, D], F32)
-        for bank in range(SLICES // 2):
-            hh = roles.tile([P, 2, DS], F32, name="hh%d" % bank)
+        diff_psum = roles.tile([P, 2, DS], F32)
+        hh_psum = gate.tile([P, 2, DS], F32, tag="gate")
+        diff_sbuf = keep.tile([P, 2, DS], F32)
+
+        def transpose_roles():
+            a_flip = flip.tile([P, SLICES, P], BF16, tag="flip")
+            for s in range(SLICES):
+                nc.tensor.transpose(a_flip[:, s, :], a_sb[:, :, s], ident_bf[:])
+            nc.scalar.copy(out=a_t[:], in_=a_flip[:])
+
+        def multiply_roles():
             for i in range(2):
-                s = 2 * bank + i
-                nc.tensor.matmul(out=hh[:, i, :], lhsT=a_t[:, s, :], rhs=vr_sb[:, s, :], start=True, stop=True)
-            cols = slice(2 * bank * DS, 2 * (bank + 1) * DS)
+                cols = slice(i * DS, (i + 1) * DS)
+                nc.tensor.matmul(out=diff_psum[:, i, :], lhsT=minus_ident[:], rhs=h_sb[:, cols], start=True, stop=False)
+                nc.tensor.matmul(out=diff_psum[:, i, :], lhsT=a_t[:, i, :], rhs=vr_sb[:, i, :], start=False, stop=True)
+            for i in range(2):
+                s = 2 + i
+                nc.tensor.matmul(out=hh_psum[:, i, :], lhsT=a_t[:, s, :], rhs=vr_sb[:, s, :], start=True, stop=True)
+
+        def subtract_h():
             nc.vector.tensor_tensor(
-                out=diff[:, cols], in0=hh[:].rearrange("b i d -> b (i d)"), in1=h_sb[:, cols], op=SUBTRACT
+                out=diff_sbuf[:].rearrange("b i d -> b (i d)"),
+                in0=hh_psum[:].rearrange("b i d -> b (i d)"),
+                in1=h_sb[:, 2 * DS :],
+                op=SUBTRACT,
             )
 
         w_codes = keep.tile([P, GROUPS, PASSES * P], U32, align_bytes=64)
@@ -120,51 +136,105 @@ def tile_tpru_pb_s_kernel(tc, a, vr, h, x2g, w_g, b_g, bg, out):
         g = keep.tile([P, D], F32)
         blend = keep.tile([P, D], F32)
         result = keep.tile([P, D], F32)
+        grouped = {}
+        sums = {}
 
-        def quantise_group(grp):
-            w_words = w_sb[grp][:].bitcast(F32)
+        def turn(grp):
             w_flip = flip.tile([P, PASSES, HALVES, P], F32, tag="flip", name="w_flip")
-            for c in range(PASSES):
-                for u in range(HALVES):
-                    words = slice(c * HALVES * P + u, (c + 1) * HALVES * P, HALVES)
-                    nc.tensor.transpose(w_flip[:, c, u, :], w_words[:, words], ident_f32[:])
+            transpose_words(w_sb[grp], w_flip)
             w_grouped = stage.tile([P, PASSES, P, PACK], BF16, align_bytes=64, name="w_grouped")
             nc.scalar.copy(out=w_grouped[:].bitcast(F32), in_=w_flip[:].rearrange("p c u o -> p c o u"))
+            grouped[grp] = w_grouped
+
+        def quantise(grp):
             nc.vector.quantize_mx(
                 out=w_codes[:, grp, :].bitcast(FP8X4),
                 scales=w_scales[:, grp, :],
-                in_=w_grouped[:].rearrange("p c o t -> p (c o t)"),
+                in_=grouped[grp][:].rearrange("p c o t -> p (c o t)"),
             )
 
-        def multiply_group(grp):
-            cols = slice(grp * P, (grp + 1) * P)
-            h2g = gate.tile([P, P], F32, name="h2g")
-            for c in range(PASSES):
-                nc.tensor.matmul_mx(
-                    out=h2g[:],
-                    lhsT=h_codes[:, c * P : (c + 1) * P].bitcast(FP8X4),
-                    lhsT_scale=h_scales[:, c * P : (c + 1) * P],
-                    rhs=w_codes[:, grp, c * P : (c + 1) * P].bitcast(FP8X4),
-                    rhs_scale=w_scales[:, grp, c * P : (c + 1) * P],
-                    start=(c == 0),
-                    stop=(c == PASSES - 1),
-                )
-            nc.vector.tensor_tensor(out=z[:, cols], in0=h2g[:], in1=pre[:, cols], op=ADD)
+        def multiply(first, count):
+            h2g = gate.tile([P, count, P], F32, tag="gate", name="h2g")
+            for i in range(count):
+                for c in range(PASSES):
+                    nc.tensor.matmul_mx(
+                        out=h2g[:, i, :],
+                        lhsT=h_codes[:, c * P : (c + 1) * P].bitcast(FP8X4),
+                        lhsT_scale=h_scales[:, c * P : (c + 1) * P],
+                        rhs=w_codes[:, first + i, c * P : (c + 1) * P].bitcast(FP8X4),
+                        rhs_scale=w_scales[:, first + i, c * P : (c + 1) * P],
+                        start=(c == 0),
+                        stop=(c == PASSES - 1),
+                    )
+            sums[first] = h2g
 
-        def blend_group(grp):
-            cols = slice(grp * P, (grp + 1) * P)
-            nc.scalar.activation(out=g[:, cols], in_=z[:, cols], func=SIGMOID)
-            nc.vector.tensor_tensor(out=blend[:, cols], in0=g[:, cols], in1=diff[:, cols], op=MULT)
+        def span(first, count):
+            return slice(first * P, (first + count) * P)
+
+        def add_pre(first, count):
+            cols = span(first, count)
+            nc.vector.tensor_tensor(
+                out=z[:, cols], in0=sums[first][:].rearrange("b i o -> b (i o)"), in1=pre[:, cols], op=ADD
+            )
+
+        def squash(first, count):
+            cols = span(first, count)
+            nc.scalar.activation(out=g[:, cols], in_=z[:, cols], func=SIGMOID, bias=bg_f32[:, 0:1])
+
+        def times_diff(first, count):
+            cols = span(first, count)
+            if first < GROUPS // 2:
+                diff = diff_psum[:].rearrange("b i d -> b (i d)")[:, cols]
+            else:
+                diff = diff_sbuf[:].rearrange("b i d -> b (i d)")[:, span(first - GROUPS // 2, count)]
+            nc.vector.tensor_tensor(out=blend[:, cols], in0=g[:, cols], in1=diff, op=MULT)
+
+        def plus_h(first, count):
+            cols = span(first, count)
             nc.vector.tensor_tensor(out=result[:, cols], in0=blend[:, cols], in1=h_sb[:, cols], op=ADD)
             nc.sync.dma_start(out=out[:, cols], in_=result[:, cols])
 
-        for rnd in range(ROUNDS + BLEND_LAG):
-            for i in range(RUN):
-                if rnd < ROUNDS:
-                    quantise_group(rnd * RUN + i)
-            for i in range(RUN):
-                if 0 <= rnd - MULTIPLY_LAG < ROUNDS:
-                    multiply_group((rnd - MULTIPLY_LAG) * RUN + i)
-            for i in range(RUN):
-                if 0 <= rnd - BLEND_LAG:
-                    blend_group((rnd - BLEND_LAG) * RUN + i)
+        transpose_roles()
+        turn(0)
+        quantise(0)
+        multiply_roles()
+        subtract_h()
+        turn(1)
+        quantise(1)
+        turn(2)
+        quantise(2)
+        turn(3)
+        quantise(3)
+        turn(4)
+        multiply(0, 2)
+        add_pre(0, 2)
+        squash(0, 2)
+        quantise(4)
+        times_diff(0, 2)
+        turn(5)
+        multiply(2, 2)
+        add_pre(2, 2)
+        quantise(5)
+        plus_h(0, 2)
+        turn(6)
+        squash(2, 2)
+        quantise(6)
+        times_diff(2, 2)
+        turn(7)
+        multiply(4, 2)
+        add_pre(4, 2)
+        squash(4, 2)
+        quantise(7)
+        plus_h(2, 2)
+        times_diff(4, 2)
+        multiply(6, 1)
+        add_pre(6, 1)
+        squash(6, 1)
+        multiply(7, 1)
+        add_pre(7, 1)
+        squash(7, 1)
+        plus_h(4, 2)
+        times_diff(6, 1)
+        times_diff(7, 1)
+        plus_h(6, 1)
+        plus_h(7, 1)

@@ -44,9 +44,9 @@ def tile_tpru_pb_s_kernel(tc, a, vr, h, x2g, w_g, b_g, bg, out):
         ctx.enter_context(tc.manual_schedule())
 
         b_runs = keep.tile([P, 2 * BIAS_WORDS], BF16)
-        nc.sync.dma_start(out=b_runs[:], in_=b_g.rearrange("(p m) -> p m", m=2 * BIAS_WORDS))
+        nc.scalar.dma_start(out=b_runs[:], in_=b_g.rearrange("(p m) -> p m", m=2 * BIAS_WORDS))
         bg_bf = keep.tile([P, 1], BF16)
-        nc.sync.dma_start(out=bg_bf[:], in_=bg.partition_broadcast(P))
+        nc.scalar.dma_start(out=bg_bf[:], in_=bg.partition_broadcast(P))
         h_sb = keep.tile([P, D], BF16)
         nc.sync.dma_start(out=h_sb[:], in_=h)
         x_sb = keep.tile([P, D], BF16)
@@ -69,20 +69,6 @@ def tile_tpru_pb_s_kernel(tc, a, vr, h, x2g, w_g, b_g, bg, out):
         minus_ident = keep.tile([P, P], BF16)
         nc.vector.tensor_scalar(out=minus_ident[:], in0=ident_bf[:], scalar1=-1.0, scalar2=None, op0=MULT)
 
-        b_words = b_runs[:].bitcast(F32)
-        bias_flip = flip.tile([P, BIAS_WORDS, P], F32, tag="flip")
-        for m in range(BIAS_WORDS):
-            nc.tensor.transpose(bias_flip[:, m, :], b_words[:, m : m + 1].to_broadcast([P, P]), ident_f32[:])
-        bg_f32 = keep.tile([P, 1], F32)
-        nc.vector.tensor_copy(out=bg_f32[:], in_=bg_bf[:])
-        pre = keep.tile([P, D], F32)
-        nc.vector.tensor_tensor(
-            out=pre[:].rearrange("b (p m e) -> b p m e", m=BIAS_WORDS, e=2),
-            in0=bias_flip[:].rearrange("b m p -> b (m p)").bitcast(BF16).rearrange("b (m p e) -> b p m e", m=BIAS_WORDS, e=2),
-            in1=x_sb[:].rearrange("b (p m e) -> b p m e", m=BIAS_WORDS, e=2),
-            op=ADD,
-        )
-
         def transpose_words(rows, banked):
             words = rows[:].bitcast(F32)
             for c in range(PASSES):
@@ -94,6 +80,18 @@ def tile_tpru_pb_s_kernel(tc, a, vr, h, x2g, w_g, b_g, bg, out):
         transpose_words(h_sb, h_flip)
         h_grouped = keep.tile([P, PASSES, P, PACK], BF16, align_bytes=64)
         nc.scalar.copy(out=h_grouped[:].bitcast(F32), in_=h_flip[:].rearrange("p c u b -> p c b u"))
+        b_words = b_runs[:].bitcast(F32)
+        bias_flip = flip.tile([P, BIAS_WORDS, P], F32, tag="flip")
+        for m in range(BIAS_WORDS):
+            nc.tensor.transpose(bias_flip[:, m, :], b_words[:, m : m + 1].to_broadcast([P, P]), ident_f32[:])
+        pre = keep.tile([P, D], F32)
+        nc.vector.tensor_tensor(
+            out=pre[:].rearrange("b (p m e) -> b p m e", m=BIAS_WORDS, e=2),
+            in0=bias_flip[:].rearrange("b m p -> b (m p)").bitcast(BF16).rearrange("b (m p e) -> b p m e", m=BIAS_WORDS, e=2),
+            in1=x_sb[:].rearrange("b (p m e) -> b p m e", m=BIAS_WORDS, e=2),
+            op=ADD,
+        )
+
         h_codes = keep.tile([P, PASSES * P], U32, align_bytes=64)
         h_scales = keep.tile([P, PASSES * P], U8, align_bytes=64)
         nc.vector.quantize_mx(
@@ -179,7 +177,7 @@ def tile_tpru_pb_s_kernel(tc, a, vr, h, x2g, w_g, b_g, bg, out):
 
         def squash(first, count):
             cols = span(first, count)
-            nc.scalar.activation(out=g[:, cols], in_=z[:, cols], func=SIGMOID, bias=bg_f32[:, 0:1])
+            nc.scalar.activation(out=g[:, cols], in_=z[:, cols], func=SIGMOID, bias=bg_bf[:, 0:1])
 
         def times_diff(first, count):
             cols = span(first, count)

@@ -33,8 +33,7 @@ def tile_tpru_pb_s_kernel(tc, a, vr, h, x2g, w_g, b_g, bg, out):
         keep = ctx.enter_context(tc.tile_pool(name="keep", bufs=1))
         stage = ctx.enter_context(tc.tile_pool(name="stage", bufs=4))
         flip = ctx.enter_context(tc.psum_pool(name="flip", bufs=4))
-        roles = ctx.enter_context(tc.psum_pool(name="roles", bufs=1))
-        gate = ctx.enter_context(tc.psum_pool(name="gate", bufs=3))
+        gate = ctx.enter_context(tc.psum_pool(name="gate", bufs=4))
 
         ident_f32 = keep.tile([P, P], F32)
         make_identity(nc, ident_f32[:])
@@ -44,30 +43,29 @@ def tile_tpru_pb_s_kernel(tc, a, vr, h, x2g, w_g, b_g, bg, out):
         ctx.enter_context(tc.manual_schedule())
 
         b_runs = keep.tile([P, 2 * BIAS_WORDS], BF16)
-        nc.scalar.dma_start(out=b_runs[:], in_=b_g.rearrange("(p m) -> p m", m=2 * BIAS_WORDS))
-        bg_bf = keep.tile([P, 1], BF16)
-        nc.scalar.dma_start(out=bg_bf[:], in_=bg.partition_broadcast(P))
+        nc.sync.dma_start(out=b_runs[:], in_=b_g.rearrange("(p m) -> p m", m=2 * BIAS_WORDS))
         h_sb = keep.tile([P, D], BF16)
         nc.sync.dma_start(out=h_sb[:], in_=h)
-        x_sb = keep.tile([P, D], BF16)
-        nc.sync.dma_start(out=x_sb[:], in_=x2g)
         a_sb = keep.tile([P, P, SLICES], BF16)
-        nc.sync.dma_start(out=a_sb[:], in_=a)
+        x_sb = keep.tile([P, D], BF16)
         vr_sb = keep.tile([P, SLICES, DS], BF16)
+        bg_bf = keep.tile([P, 1], BF16)
         w_sb = []
         for grp in range(GROUPS):
             w_rows = keep.tile([P, D], BF16, name="w_rows%d" % grp)
             nc.sync.dma_start(out=w_rows[:], in_=w_g[grp * P : (grp + 1) * P, :])
             w_sb.append(w_rows)
             if grp == 0:
+                nc.sync.dma_start(out=a_sb[:], in_=a)
+                nc.sync.dma_start(out=x_sb[:], in_=x2g)
+            if grp == 1:
                 nc.sync.dma_start(out=vr_sb[:], in_=vr)
+                nc.sync.dma_start(out=bg_bf[:], in_=bg.partition_broadcast(P))
 
         zero_col = keep.tile([P, 1], F32)
         nc.vector.memset(zero_col[:], 0.0)
         half_col = keep.tile([P, 1], F32)
         nc.scalar.activation(out=half_col[:], in_=zero_col[:], func=SIGMOID)
-        minus_ident = keep.tile([P, P], BF16)
-        nc.vector.tensor_scalar(out=minus_ident[:], in0=ident_bf[:], scalar1=-1.0, scalar2=None, op0=MULT)
 
         def transpose_words(rows, banked):
             words = rows[:].bitcast(F32)
@@ -76,22 +74,14 @@ def tile_tpru_pb_s_kernel(tc, a, vr, h, x2g, w_g, b_g, bg, out):
                     picked = slice(c * HALVES * P + u, (c + 1) * HALVES * P, HALVES)
                     nc.tensor.transpose(banked[:, c, u, :], words[:, picked], ident_f32[:])
 
+        b_words = b_runs[:].bitcast(F32)
+        bias_flip = gate.tile([P, BIAS_WORDS, P], F32, tag="gate")
+        for m in range(BIAS_WORDS):
+            nc.tensor.transpose(bias_flip[:, m, :], b_words[:, m : m + 1].to_broadcast([P, P]), ident_f32[:])
         h_flip = flip.tile([P, PASSES, HALVES, P], F32, tag="flip")
         transpose_words(h_sb, h_flip)
         h_grouped = keep.tile([P, PASSES, P, PACK], BF16, align_bytes=64)
         nc.scalar.copy(out=h_grouped[:].bitcast(F32), in_=h_flip[:].rearrange("p c u b -> p c b u"))
-        b_words = b_runs[:].bitcast(F32)
-        bias_flip = flip.tile([P, BIAS_WORDS, P], F32, tag="flip")
-        for m in range(BIAS_WORDS):
-            nc.tensor.transpose(bias_flip[:, m, :], b_words[:, m : m + 1].to_broadcast([P, P]), ident_f32[:])
-        pre = keep.tile([P, D], F32)
-        nc.vector.tensor_tensor(
-            out=pre[:].rearrange("b (p m e) -> b p m e", m=BIAS_WORDS, e=2),
-            in0=bias_flip[:].rearrange("b m p -> b (m p)").bitcast(BF16).rearrange("b (m p e) -> b p m e", m=BIAS_WORDS, e=2),
-            in1=x_sb[:].rearrange("b (p m e) -> b p m e", m=BIAS_WORDS, e=2),
-            op=ADD,
-        )
-
         h_codes = keep.tile([P, PASSES * P], U32, align_bytes=64)
         h_scales = keep.tile([P, PASSES * P], U8, align_bytes=64)
         nc.vector.quantize_mx(
@@ -100,10 +90,17 @@ def tile_tpru_pb_s_kernel(tc, a, vr, h, x2g, w_g, b_g, bg, out):
             in_=h_grouped[:].rearrange("p c b t -> p (c b t)"),
         )
 
+        pre = keep.tile([P, D], F32)
+        nc.vector.tensor_tensor(
+            out=pre[:].rearrange("b (p m e) -> b p m e", m=BIAS_WORDS, e=2),
+            in0=bias_flip[:].rearrange("b m p -> b (m p)").bitcast(BF16).rearrange("b (m p e) -> b p m e", m=BIAS_WORDS, e=2),
+            in1=x_sb[:].rearrange("b (p m e) -> b p m e", m=BIAS_WORDS, e=2),
+            op=ADD,
+        )
+
         a_t = keep.tile([P, SLICES, P], BF16)
-        diff_psum = roles.tile([P, 2, DS], F32)
-        hh_psum = gate.tile([P, 2, DS], F32, tag="gate")
-        diff_sbuf = keep.tile([P, 2, DS], F32)
+        diff = keep.tile([P, D], F32)
+        hh_banks = []
 
         def transpose_roles():
             a_flip = flip.tile([P, SLICES, P], BF16, tag="flip")
@@ -111,21 +108,17 @@ def tile_tpru_pb_s_kernel(tc, a, vr, h, x2g, w_g, b_g, bg, out):
                 nc.tensor.transpose(a_flip[:, s, :], a_sb[:, :, s], ident_bf[:])
             nc.scalar.copy(out=a_t[:], in_=a_flip[:])
 
-        def multiply_roles():
+        def multiply_roles(bank):
+            hh = gate.tile([P, 2, DS], F32, tag="gate", name="hh")
             for i in range(2):
-                cols = slice(i * DS, (i + 1) * DS)
-                nc.tensor.matmul(out=diff_psum[:, i, :], lhsT=minus_ident[:], rhs=h_sb[:, cols], start=True, stop=False)
-                nc.tensor.matmul(out=diff_psum[:, i, :], lhsT=a_t[:, i, :], rhs=vr_sb[:, i, :], start=False, stop=True)
-            for i in range(2):
-                s = 2 + i
-                nc.tensor.matmul(out=hh_psum[:, i, :], lhsT=a_t[:, s, :], rhs=vr_sb[:, s, :], start=True, stop=True)
+                s = 2 * bank + i
+                nc.tensor.matmul(out=hh[:, i, :], lhsT=a_t[:, s, :], rhs=vr_sb[:, s, :], start=True, stop=True)
+            hh_banks.append(hh)
 
-        def subtract_h():
+        def subtract_h(bank):
+            cols = slice(2 * bank * DS, 2 * (bank + 1) * DS)
             nc.vector.tensor_tensor(
-                out=diff_sbuf[:].rearrange("b i d -> b (i d)"),
-                in0=hh_psum[:].rearrange("b i d -> b (i d)"),
-                in1=h_sb[:, 2 * DS :],
-                op=SUBTRACT,
+                out=diff[:, cols], in0=hh_banks[bank][:].rearrange("b i d -> b (i d)"), in1=h_sb[:, cols], op=SUBTRACT
             )
 
         w_codes = keep.tile([P, GROUPS, PASSES * P], U32, align_bytes=64)
@@ -181,56 +174,52 @@ def tile_tpru_pb_s_kernel(tc, a, vr, h, x2g, w_g, b_g, bg, out):
 
         def times_diff(first, count):
             cols = span(first, count)
-            if first < GROUPS // 2:
-                diff = diff_psum[:].rearrange("b i d -> b (i d)")[:, cols]
-            else:
-                diff = diff_sbuf[:].rearrange("b i d -> b (i d)")[:, span(first - GROUPS // 2, count)]
-            nc.vector.tensor_tensor(out=blend[:, cols], in0=g[:, cols], in1=diff, op=MULT)
+            nc.vector.tensor_tensor(out=blend[:, cols], in0=g[:, cols], in1=diff[:, cols], op=MULT)
 
         def plus_h(first, count):
             cols = span(first, count)
             nc.vector.tensor_tensor(out=result[:, cols], in0=blend[:, cols], in1=h_sb[:, cols], op=ADD)
             nc.sync.dma_start(out=out[:, cols], in_=result[:, cols])
 
-        transpose_roles()
         turn(0)
-        quantise(0)
-        multiply_roles()
-        subtract_h()
+        transpose_roles()
         turn(1)
+        multiply_roles(0)
+        multiply_roles(1)
+        subtract_h(0)
+        quantise(0)
         quantise(1)
+        subtract_h(1)
         turn(2)
         quantise(2)
         turn(3)
         quantise(3)
         turn(4)
+        quantise(4)
+        turn(5)
         multiply(0, 2)
         add_pre(0, 2)
+        quantise(5)
+        turn(6)
         squash(0, 2)
-        quantise(4)
-        times_diff(0, 2)
-        turn(5)
         multiply(2, 2)
         add_pre(2, 2)
-        quantise(5)
-        plus_h(0, 2)
-        turn(6)
-        squash(2, 2)
         quantise(6)
-        times_diff(2, 2)
+        times_diff(0, 2)
         turn(7)
+        squash(2, 2)
         multiply(4, 2)
         add_pre(4, 2)
         squash(4, 2)
         quantise(7)
-        plus_h(2, 2)
+        times_diff(2, 2)
+        plus_h(0, 2)
+        multiply(6, 2)
         times_diff(4, 2)
-        multiply(6, 1)
-        add_pre(6, 1)
+        add_pre(6, 2)
         squash(6, 1)
-        multiply(7, 1)
-        add_pre(7, 1)
         squash(7, 1)
+        plus_h(2, 2)
         plus_h(4, 2)
         times_diff(6, 1)
         times_diff(7, 1)

@@ -49,7 +49,8 @@ def tile_tpru_pb_s_kernel(tc, a, vr, h, x2g, w_g, b_g, bg, out):
         a_sb = keep.tile([P, P, SLICES], BF16)
         x_sb = keep.tile([P, D], BF16)
         vr_sb = keep.tile([P, SLICES, DS], BF16)
-        bg_bf = keep.tile([P, 1], BF16)
+        bg_runs = keep.tile([P, 2], BF16)
+        nc.vector.memset(bg_runs[:], 0.0)
         w_sb = []
         for grp in range(GROUPS):
             w_rows = keep.tile([P, D], BF16, name="w_rows%d" % grp)
@@ -60,7 +61,7 @@ def tile_tpru_pb_s_kernel(tc, a, vr, h, x2g, w_g, b_g, bg, out):
                 nc.sync.dma_start(out=x_sb[:], in_=x2g)
             if grp == 1:
                 nc.sync.dma_start(out=vr_sb[:], in_=vr)
-                nc.sync.dma_start(out=bg_bf[:], in_=bg.partition_broadcast(P))
+                nc.sync.dma_start(out=bg_runs[0:1, 0:1], in_=bg.rearrange("(o n) -> o n", o=1))
 
         zero_col = keep.tile([P, 1], F32)
         nc.vector.memset(zero_col[:], 0.0)
@@ -97,6 +98,13 @@ def tile_tpru_pb_s_kernel(tc, a, vr, h, x2g, w_g, b_g, bg, out):
             in1=x_sb[:].rearrange("b (p m e) -> b p m e", m=BIAS_WORDS, e=2),
             op=ADD,
         )
+
+        bg_f32 = keep.tile([P, 1], F32)
+
+        def spread_bg():
+            bg_flip = gate.tile([P, P], F32, tag="gate")
+            nc.tensor.transpose(bg_flip[:], bg_runs[:].bitcast(F32).to_broadcast([P, P]), ident_f32[:])
+            nc.vector.tensor_copy(out=bg_f32[:], in_=bg_flip[:].bitcast(BF16)[:, 0:1])
 
         a_t = keep.tile([P, SLICES, P], BF16)
         diff = keep.tile([P, D], F32)
@@ -170,7 +178,7 @@ def tile_tpru_pb_s_kernel(tc, a, vr, h, x2g, w_g, b_g, bg, out):
 
         def squash(first, count):
             cols = span(first, count)
-            nc.scalar.activation(out=g[:, cols], in_=z[:, cols], func=SIGMOID, bias=bg_bf[:, 0:1])
+            nc.scalar.activation(out=g[:, cols], in_=z[:, cols], func=SIGMOID, bias=bg_f32[:, 0:1])
 
         def times_diff(first, count):
             cols = span(first, count)
@@ -190,6 +198,7 @@ def tile_tpru_pb_s_kernel(tc, a, vr, h, x2g, w_g, b_g, bg, out):
         quantise(0)
         quantise(1)
         subtract_h(1)
+        spread_bg()
         turn(2)
         quantise(2)
         turn(3)

@@ -7,6 +7,7 @@ F32 = mybir.dt.float32
 BF16 = mybir.dt.bfloat16
 U32 = mybir.dt.uint32
 U8 = mybir.dt.uint8
+I32 = mybir.dt.int32
 FP8X4 = mybir.dt.float8_e4m3fn_x4
 ADD = mybir.AluOpType.add
 SUBTRACT = mybir.AluOpType.subtract
@@ -23,6 +24,9 @@ PASSES = D // K_PASS
 HALVES = 2
 GROUPS = D // P
 BIAS_WORDS = D // P // 2
+
+IDLE_COLS = 256
+PAIR_OF_ONES = 0x3F803F80
 
 FLOPS = 2 * P * D * D + 2 * P * P * D
 
@@ -62,6 +66,27 @@ def tile_tpru_pb_s_kernel(tc, a, vr, h, x2g, w_g, b_g, bg, out):
             if grp == 1:
                 nc.sync.dma_start(out=vr_sb[:], in_=vr)
                 nc.sync.dma_start(out=bg_runs[0:1, 0:1], in_=bg.rearrange("(o n) -> o n", o=1))
+
+        ones = keep.tile([P, PACK * IDLE_COLS], BF16, align_bytes=64)
+        nc.vector.memset(ones[:].bitcast(I32), PAIR_OF_ONES)
+        ones_codes = keep.tile([P, IDLE_COLS], U32, align_bytes=64)
+        ones_scales = keep.tile([P, IDLE_COLS], U8, align_bytes=64)
+        nc.vector.quantize_mx(out=ones_codes[:].bitcast(FP8X4), scales=ones_scales[:], in_=ones[:])
+
+        def keep_awake(passes):
+            unread = gate.tile([P, IDLE_COLS], F32, tag="gate", name="unread")
+            for i in range(passes):
+                nc.tensor.matmul_mx(
+                    out=unread[:],
+                    lhsT=ones_codes[:, :P].bitcast(FP8X4),
+                    lhsT_scale=ones_scales[:, :P],
+                    rhs=ones_codes[:].bitcast(FP8X4),
+                    rhs_scale=ones_scales[:],
+                    start=True,
+                    stop=True,
+                )
+
+        keep_awake(6)
 
         zero_col = keep.tile([P, 1], F32)
         nc.vector.memset(zero_col[:], 0.0)
@@ -191,6 +216,7 @@ def tile_tpru_pb_s_kernel(tc, a, vr, h, x2g, w_g, b_g, bg, out):
 
         turn(0)
         transpose_roles()
+        keep_awake(3)
         turn(1)
         multiply_roles(0)
         multiply_roles(1)

@@ -25,7 +25,7 @@ HALVES = 2
 GROUPS = D // P
 BIAS_WORDS = D // P // 2
 
-IDLE_COLS = 256
+IDLE_COLS = 128
 PAIR_OF_ONES = 0x3F803F80
 
 FLOPS = 2 * P * D * D + 2 * P * P * D
@@ -86,7 +86,7 @@ def tile_tpru_pb_s_kernel(tc, a, vr, h, x2g, w_g, b_g, bg, out):
                     stop=True,
                 )
 
-        keep_awake(6)
+        keep_awake(12)
 
         zero_col = keep.tile([P, 1], F32)
         nc.vector.memset(zero_col[:], 0.0)
@@ -214,14 +214,14 @@ def tile_tpru_pb_s_kernel(tc, a, vr, h, x2g, w_g, b_g, bg, out):
             nc.vector.tensor_tensor(out=result[:, cols], in0=blend[:, cols], in1=h_sb[:, cols], op=ADD)
             nc.sync.dma_start(out=out[:, cols], in_=result[:, cols])
 
-        turn(0)
         transpose_roles()
-        keep_awake(3)
+        turn(0)
+        keep_awake(6)
+        quantise(0)
         turn(1)
         multiply_roles(0)
         multiply_roles(1)
         subtract_h(0)
-        quantise(0)
         quantise(1)
         subtract_h(1)
         spread_bg()
@@ -230,33 +230,33 @@ def tile_tpru_pb_s_kernel(tc, a, vr, h, x2g, w_g, b_g, bg, out):
         turn(3)
         quantise(3)
         turn(4)
-        quantise(4)
         turn(5)
         multiply(0, 2)
         add_pre(0, 2)
-        quantise(5)
-        turn(6)
+        quantise(4)
         squash(0, 2)
         multiply(2, 2)
-        add_pre(2, 2)
-        quantise(6)
+        quantise(5)
         times_diff(0, 2)
+        add_pre(2, 2)
+        turn(6)
+        plus_h(0, 2)
+        quantise(6)
         turn(7)
+        quantise(7)
         squash(2, 2)
+        times_diff(2, 2)
         multiply(4, 2)
         add_pre(4, 2)
         squash(4, 2)
-        quantise(7)
-        times_diff(2, 2)
-        plus_h(0, 2)
         multiply(6, 2)
-        times_diff(4, 2)
         add_pre(6, 2)
         squash(6, 1)
         squash(7, 1)
         plus_h(2, 2)
-        plus_h(4, 2)
+        times_diff(4, 2)
         times_diff(6, 1)
         times_diff(7, 1)
+        plus_h(4, 2)
         plus_h(6, 1)
         plus_h(7, 1)

@@ -58,7 +58,12 @@ def tile_tpru_pb_s_kernel(tc, a, vr, h, x2g, w_g, b_g, bg, out):
         w_sb = []
         for grp in range(GROUPS):
             w_rows = keep.tile([P, D], BF16, name="w_rows%d" % grp)
-            nc.sync.dma_start(out=w_rows[:], in_=w_g[grp * P : (grp + 1) * P, :])
+            if grp < GROUPS - 1:
+                nc.sync.dma_start(out=w_rows[:], in_=w_g[grp * P : (grp + 1) * P, :])
+            else:
+                for c in range(PASSES):
+                    ks = slice(c * K_PASS, (c + 1) * K_PASS)
+                    nc.sync.dma_start(out=w_rows[:, ks], in_=w_g[grp * P : (grp + 1) * P, ks])
             w_sb.append(w_rows)
             if grp == 0:
                 nc.sync.dma_start(out=a_sb[:], in_=a)
@@ -73,8 +78,9 @@ def tile_tpru_pb_s_kernel(tc, a, vr, h, x2g, w_g, b_g, bg, out):
         ones_scales = keep.tile([P, IDLE_COLS], U8, align_bytes=64)
         nc.vector.quantize_mx(out=ones_codes[:].bitcast(FP8X4), scales=ones_scales[:], in_=ones[:])
 
+        unread = gate.tile([P, IDLE_COLS], F32, tag="gate")
+
         def keep_awake(passes):
-            unread = gate.tile([P, IDLE_COLS], F32, tag="gate", name="unread")
             for i in range(passes):
                 nc.tensor.matmul_mx(
                     out=unread[:],
@@ -177,6 +183,24 @@ def tile_tpru_pb_s_kernel(tc, a, vr, h, x2g, w_g, b_g, bg, out):
                 in_=grouped[grp][:].rearrange("p c o t -> p (c o t)"),
             )
 
+        def turn_pass(grp, c):
+            half_flip = flip.tile([P, HALVES, P], F32, tag="flip", name="half_flip")
+            words = w_sb[grp][:].bitcast(F32)
+            for u in range(HALVES):
+                picked = slice(c * HALVES * P + u, (c + 1) * HALVES * P, HALVES)
+                nc.tensor.transpose(half_flip[:, u, :], words[:, picked], ident_f32[:])
+            half_grouped = stage.tile([P, P, PACK], BF16, align_bytes=64, name="half_grouped")
+            nc.scalar.copy(out=half_grouped[:].bitcast(F32), in_=half_flip[:].rearrange("p u o -> p o u"))
+            grouped[grp, c] = half_grouped
+
+        def quantise_pass(grp, c):
+            cols = slice(c * P, (c + 1) * P)
+            nc.vector.quantize_mx(
+                out=w_codes[:, grp, cols].bitcast(FP8X4),
+                scales=w_scales[:, grp, cols],
+                in_=grouped[grp, c][:].rearrange("p o t -> p (o t)"),
+            )
+
         def multiply(first, count):
             h2g = gate.tile([P, count, P], F32, tag="gate", name="h2g")
             for i in range(count):
@@ -242,21 +266,25 @@ def tile_tpru_pb_s_kernel(tc, a, vr, h, x2g, w_g, b_g, bg, out):
         turn(6)
         plus_h(0, 2)
         quantise(6)
-        turn(7)
-        quantise(7)
-        squash(2, 2)
-        times_diff(2, 2)
+        turn_pass(7, 0)
+        turn_pass(7, 1)
         multiply(4, 2)
+        squash(2, 2)
         add_pre(4, 2)
         squash(4, 2)
-        multiply(6, 2)
-        add_pre(6, 2)
+        quantise_pass(7, 0)
+        quantise_pass(7, 1)
+        multiply(6, 1)
+        times_diff(2, 2)
+        add_pre(6, 1)
         squash(6, 1)
-        squash(7, 1)
+        multiply(7, 1)
         plus_h(2, 2)
+        add_pre(7, 1)
+        squash(7, 1)
         times_diff(4, 2)
         times_diff(6, 1)
-        times_diff(7, 1)
         plus_h(4, 2)
+        times_diff(7, 1)
         plus_h(6, 1)
         plus_h(7, 1)

from contextlib import ExitStack

import concourse.mybir as mybir
from concourse.masks import make_identity

F32 = mybir.dt.float32
BF16 = mybir.dt.bfloat16
U32 = mybir.dt.uint32
U8 = mybir.dt.uint8
I32 = mybir.dt.int32
FP8X4 = mybir.dt.float8_e4m3fn_x4
ADD = mybir.AluOpType.add
SUBTRACT = mybir.AluOpType.subtract
MULT = mybir.AluOpType.mult
SIGMOID = mybir.ActivationFunctionType.Sigmoid

P = 128
D = 1024
SLICES = 4
DS = D // SLICES
PACK = 4
K_PASS = P * PACK
PASSES = D // K_PASS
HALVES = 2
GROUPS = D // P
BIAS_WORDS = D // P // 2

IDLE_COLS = 128
PAIR_OF_ONES = 0x3F803F80

FLOPS = 2 * P * D * D + 2 * P * P * D


def tile_tpru_pb_s_kernel(tc, a, vr, h, x2g, w_g, b_g, bg, out):
    nc = tc.nc
    with ExitStack() as ctx:
        keep = ctx.enter_context(tc.tile_pool(name="keep", bufs=1))
        stage = ctx.enter_context(tc.tile_pool(name="stage", bufs=4))
        flip = ctx.enter_context(tc.psum_pool(name="flip", bufs=4))
        gate = ctx.enter_context(tc.psum_pool(name="gate", bufs=4))

        ident_f32 = keep.tile([P, P], F32)
        make_identity(nc, ident_f32[:])
        ident_bf = keep.tile([P, P], BF16)
        make_identity(nc, ident_bf[:])

        ctx.enter_context(tc.manual_schedule())

        b_runs = keep.tile([P, 2 * BIAS_WORDS], BF16)
        nc.sync.dma_start(out=b_runs[:], in_=b_g.rearrange("(p m) -> p m", m=2 * BIAS_WORDS))
        h_sb = keep.tile([P, D], BF16)
        nc.sync.dma_start(out=h_sb[:], in_=h)
        a_sb = keep.tile([P, P, SLICES], BF16)
        x_sb = keep.tile([P, D], BF16)
        vr_sb = keep.tile([P, SLICES, DS], BF16)
        bg_runs = keep.tile([P, 2], BF16)
        nc.vector.memset(bg_runs[:], 0.0)
        w_sb = []
        for grp in range(GROUPS):
            w_rows = keep.tile([P, D], BF16, name="w_rows%d" % grp)
            if grp < GROUPS - 1:
                nc.sync.dma_start(out=w_rows[:], in_=w_g[grp * P : (grp + 1) * P, :])
            else:
                for c in range(PASSES):
                    ks = slice(c * K_PASS, (c + 1) * K_PASS)
                    nc.sync.dma_start(out=w_rows[:, ks], in_=w_g[grp * P : (grp + 1) * P, ks])
            w_sb.append(w_rows)
            if grp == 0:
                nc.sync.dma_start(out=a_sb[:], in_=a)
                nc.sync.dma_start(out=x_sb[:], in_=x2g)
            if grp == 1:
                nc.sync.dma_start(out=vr_sb[:], in_=vr)
                nc.sync.dma_start(out=bg_runs[0:1, 0:1], in_=bg.rearrange("(o n) -> o n", o=1))

        ones = keep.tile([P, PACK * IDLE_COLS], BF16, align_bytes=64)
        nc.vector.memset(ones[:].bitcast(I32), PAIR_OF_ONES)
        ones_codes = keep.tile([P, IDLE_COLS], U32, align_bytes=64)
        ones_scales = keep.tile([P, IDLE_COLS], U8, align_bytes=64)
        nc.vector.quantize_mx(out=ones_codes[:].bitcast(FP8X4), scales=ones_scales[:], in_=ones[:])

        unread = gate.tile([P, IDLE_COLS], F32, tag="gate")

        def keep_awake(passes):
            for i in range(passes):
                nc.tensor.matmul_mx(
                    out=unread[:],
                    lhsT=ones_codes[:, :P].bitcast(FP8X4),
                    lhsT_scale=ones_scales[:, :P],
                    rhs=ones_codes[:].bitcast(FP8X4),
                    rhs_scale=ones_scales[:],
                    start=True,
                    stop=True,
                )

        keep_awake(12)

        zero_col = keep.tile([P, 1], F32)
        nc.vector.memset(zero_col[:], 0.0)
        half_col = keep.tile([P, 1], F32)
        nc.scalar.activation(out=half_col[:], in_=zero_col[:], func=SIGMOID)

        def transpose_words(rows, banked):
            words = rows[:].bitcast(F32)
            for c in range(PASSES):
                for u in range(HALVES):
                    picked = slice(c * HALVES * P + u, (c + 1) * HALVES * P, HALVES)
                    nc.tensor.transpose(banked[:, c, u, :], words[:, picked], ident_f32[:])

        b_words = b_runs[:].bitcast(F32)
        bias_flip = gate.tile([P, BIAS_WORDS, P], F32, tag="gate")
        for m in range(BIAS_WORDS):
            nc.tensor.transpose(bias_flip[:, m, :], b_words[:, m : m + 1].to_broadcast([P, P]), ident_f32[:])
        h_flip = flip.tile([P, PASSES, HALVES, P], F32, tag="flip")
        transpose_words(h_sb, h_flip)
        h_grouped = keep.tile([P, PASSES, P, PACK], BF16, align_bytes=64)
        nc.scalar.copy(out=h_grouped[:].bitcast(F32), in_=h_flip[:].rearrange("p c u b -> p c b u"))
        h_codes = keep.tile([P, PASSES * P], U32, align_bytes=64)
        h_scales = keep.tile([P, PASSES * P], U8, align_bytes=64)
        nc.vector.quantize_mx(
            out=h_codes[:].bitcast(FP8X4),
            scales=h_scales[:],
            in_=h_grouped[:].rearrange("p c b t -> p (c b t)"),
        )

        pre = keep.tile([P, D], F32)
        nc.vector.tensor_tensor(
            out=pre[:].rearrange("b (p m e) -> b p m e", m=BIAS_WORDS, e=2),
            in0=bias_flip[:].rearrange("b m p -> b (m p)").bitcast(BF16).rearrange("b (m p e) -> b p m e", m=BIAS_WORDS, e=2),
            in1=x_sb[:].rearrange("b (p m e) -> b p m e", m=BIAS_WORDS, e=2),
            op=ADD,
        )

        bg_f32 = keep.tile([P, 1], F32)

        def spread_bg():
            bg_flip = gate.tile([P, P], F32, tag="gate")
            nc.tensor.transpose(bg_flip[:], bg_runs[:].bitcast(F32).to_broadcast([P, P]), ident_f32[:])
            nc.vector.tensor_copy(out=bg_f32[:], in_=bg_flip[:].bitcast(BF16)[:, 0:1])

        a_t = keep.tile([P, SLICES, P], BF16)
        diff = keep.tile([P, D], F32)
        hh_banks = []

        def transpose_roles():
            a_flip = flip.tile([P, SLICES, P], BF16, tag="flip")
            for s in range(SLICES):
                nc.tensor.transpose(a_flip[:, s, :], a_sb[:, :, s], ident_bf[:])
            nc.scalar.copy(out=a_t[:], in_=a_flip[:])

        def multiply_roles(bank):
            hh = gate.tile([P, 2, DS], F32, tag="gate", name="hh")
            for i in range(2):
                s = 2 * bank + i
                nc.tensor.matmul(out=hh[:, i, :], lhsT=a_t[:, s, :], rhs=vr_sb[:, s, :], start=True, stop=True)
            hh_banks.append(hh)

        def subtract_h(bank):
            cols = slice(2 * bank * DS, 2 * (bank + 1) * DS)
            nc.vector.tensor_tensor(
                out=diff[:, cols], in0=hh_banks[bank][:].rearrange("b i d -> b (i d)"), in1=h_sb[:, cols], op=SUBTRACT
            )

        w_codes = keep.tile([P, GROUPS, PASSES * P], U32, align_bytes=64)
        w_scales = keep.tile([P, GROUPS, PASSES * P], U8, align_bytes=64)
        z = keep.tile([P, D], F32)
        g = keep.tile([P, D], F32)
        blend = keep.tile([P, D], F32)
        result = keep.tile([P, D], F32)
        grouped = {}
        sums = {}

        def turn(grp):
            w_flip = flip.tile([P, PASSES, HALVES, P], F32, tag="flip", name="w_flip")
            transpose_words(w_sb[grp], w_flip)
            w_grouped = stage.tile([P, PASSES, P, PACK], BF16, align_bytes=64, name="w_grouped")
            nc.scalar.copy(out=w_grouped[:].bitcast(F32), in_=w_flip[:].rearrange("p c u o -> p c o u"))
            grouped[grp] = w_grouped

        def quantise(grp):
            nc.vector.quantize_mx(
                out=w_codes[:, grp, :].bitcast(FP8X4),
                scales=w_scales[:, grp, :],
                in_=grouped[grp][:].rearrange("p c o t -> p (c o t)"),
            )

        def turn_pass(grp, c):
            half_flip = flip.tile([P, HALVES, P], F32, tag="flip", name="half_flip")
            words = w_sb[grp][:].bitcast(F32)
            for u in range(HALVES):
                picked = slice(c * HALVES * P + u, (c + 1) * HALVES * P, HALVES)
                nc.tensor.transpose(half_flip[:, u, :], words[:, picked], ident_f32[:])
            half_grouped = stage.tile([P, P, PACK], BF16, align_bytes=64, name="half_grouped")
            nc.scalar.copy(out=half_grouped[:].bitcast(F32), in_=half_flip[:].rearrange("p u o -> p o u"))
            grouped[grp, c] = half_grouped

        def quantise_pass(grp, c):
            cols = slice(c * P, (c + 1) * P)
            nc.vector.quantize_mx(
                out=w_codes[:, grp, cols].bitcast(FP8X4),
                scales=w_scales[:, grp, cols],
                in_=grouped[grp, c][:].rearrange("p o t -> p (o t)"),
            )

        def multiply(first, count):
            h2g = gate.tile([P, count, P], F32, tag="gate", name="h2g")
            for i in range(count):
                for c in range(PASSES):
                    nc.tensor.matmul_mx(
                        out=h2g[:, i, :],
                        lhsT=h_codes[:, c * P : (c + 1) * P].bitcast(FP8X4),
                        lhsT_scale=h_scales[:, c * P : (c + 1) * P],
                        rhs=w_codes[:, first + i, c * P : (c + 1) * P].bitcast(FP8X4),
                        rhs_scale=w_scales[:, first + i, c * P : (c + 1) * P],
                        start=(c == 0),
                        stop=(c == PASSES - 1),
                    )
            sums[first] = h2g

        def span(first, count):
            return slice(first * P, (first + count) * P)

        def add_pre(first, count):
            cols = span(first, count)
            nc.vector.tensor_tensor(
                out=z[:, cols], in0=sums[first][:].rearrange("b i o -> b (i o)"), in1=pre[:, cols], op=ADD
            )

        def squash(first, count):
            cols = span(first, count)
            nc.scalar.activation(out=g[:, cols], in_=z[:, cols], func=SIGMOID, bias=bg_f32[:, 0:1])

        def times_diff(first, count):
            cols = span(first, count)
            nc.vector.tensor_tensor(out=blend[:, cols], in0=g[:, cols], in1=diff[:, cols], op=MULT)

        def plus_h(first, count):
            cols = span(first, count)
            nc.vector.tensor_tensor(out=result[:, cols], in0=blend[:, cols], in1=h_sb[:, cols], op=ADD)
            nc.sync.dma_start(out=out[:, cols], in_=result[:, cols])

        transpose_roles()
        turn(0)
        keep_awake(6)
        quantise(0)
        turn(1)
        multiply_roles(0)
        multiply_roles(1)
        subtract_h(0)
        quantise(1)
        subtract_h(1)
        spread_bg()
        turn(2)
        quantise(2)
        turn(3)
        quantise(3)
        turn(4)
        turn(5)
        multiply(0, 2)
        add_pre(0, 2)
        quantise(4)
        squash(0, 2)
        multiply(2, 2)
        quantise(5)
        times_diff(0, 2)
        add_pre(2, 2)
        turn(6)
        plus_h(0, 2)
        quantise(6)
        turn_pass(7, 0)
        turn_pass(7, 1)
        multiply(4, 2)
        squash(2, 2)
        add_pre(4, 2)
        squash(4, 2)
        quantise_pass(7, 0)
        quantise_pass(7, 1)
        multiply(6, 1)
        times_diff(2, 2)
        add_pre(6, 1)
        squash(6, 1)
        multiply(7, 1)
        plus_h(2, 2)
        add_pre(7, 1)
        squash(7, 1)
        times_diff(4, 2)
        times_diff(6, 1)
        plus_h(4, 2)
        times_diff(7, 1)
        plus_h(6, 1)
        plus_h(7, 1)
